import numpy as np
import ml_dtypes


def mxq(x, axis, fmt="e4m3"):
    dtype, down = {"e4m3": (ml_dtypes.float8_e4m3fn, 7), "e5m2": (ml_dtypes.float8_e5m2, 14)}[fmt]
    v = np.moveaxis(np.asarray(x, np.float32).astype(ml_dtypes.bfloat16).astype(np.float64), axis, -1)
    blocks = v.reshape(v.shape[:-1] + (-1, 32))
    amax = np.abs(blocks).max(-1, keepdims=True)
    byte = np.maximum(np.where(amax > 0, np.frexp(amax)[1] - 1 + 127, 0) - down, 1)
    scale = np.exp2(byte - 127.0)
    codes = (blocks / scale).astype(np.float32).astype(dtype).astype(np.float64)
    return np.moveaxis((codes * scale).reshape(v.shape), -1, axis)


WIDE = False


def mx_kscale(k):
    if not WIDE:
        return np.ones(k)
    levels = np.array([10, -10, 5, -5, 0])
    a = np.random.permutation(np.resize(levels, k // 512 * 4)).reshape(k // 512, 4)
    idx = np.arange(k)
    return np.exp2(a[idx // 512, idx % 128 // 32])


BF16 = ml_dtypes.bfloat16


def bf(x):
    return np.asarray(x, np.float32).astype(BF16)


def f64(x):
    return np.asarray(x).astype(np.float64)


B, DH, DO, L = 1024, 2048, 1024, 128


def setup_inputs():
    s = mx_kscale(2 * DH)
    t = mx_kscale(DO)
    return {"sbj_vec": bf(np.random.standard_normal((B, DH)) * s[:DH]),
            "obj_vec": bf(np.random.standard_normal((B, DH)) * s[DH:]),
            "W1": bf(np.random.standard_normal((2 * DH, DO)) * 1.28 / np.sqrt(2 * DH) / s[:, None] * t),
            "b1": bf(np.random.standard_normal(DO) * 0.1 * t),
            "W2": bf(np.random.standard_normal((DO, DO)) * 12.0 / DO / t[:, None]),
            "b2": bf(np.random.standard_normal(DO) * 0.1),
            "label_vecs": bf(np.random.standard_normal((L, DO)) * 8.0 / np.sqrt(DO))}


def reference(sbj_vec, obj_vec, W1, b1, W2, b2, label_vecs):
    x = np.concatenate([f64(sbj_vec), f64(obj_vec)], axis=1)
    hidden = (mxq(np.maximum(x, 0.0), 1, "e4m3") @ mxq(f64(W1), 0, "e4m3")) + f64(b1)
    emb = (mxq(np.maximum(hidden, 0.0), 1, "e4m3") @ mxq(f64(W2), 0, "e4m3")) + f64(b2)
    lab = f64(label_vecs)
    scores = np.empty((emb.shape[0], lab.shape[0]))
    for l in range(lab.shape[0]):
        diff = np.maximum(lab[l][None, :] - emb, 0.0)
        scores[:, l] = -np.sqrt(np.sum(diff * diff, axis=1))
    return scores

@@ -1,0 +1,250 @@
+import concourse.mybir as mybir
+from concourse.masks import make_identity
+
+F32 = mybir.dt.float32
+BF16 = mybir.dt.bfloat16
+U32 = mybir.dt.uint32
+U8 = mybir.dt.uint8
+FP8X4 = mybir.dt.float8_e4m3fn_x4
+ALU = mybir.AluOpType
+ACT = mybir.ActivationFunctionType
+AX = mybir.AxisListType
+
+P = 128
+B, DH, DO, L = 1024, 2048, 1024, 128
+PACK = 4
+KPASS = P * PACK
+G1 = 2 * DH // KPASS
+G2 = DO // KPASS
+NB = B // P
+HB = 512
+NH = B // HB
+NO = DO // P
+
+FLOPS = 2 * B * 2 * DH * DO + 2 * B * DO * DO + 4 * B * L * DO
+
+KEEP_EVERY = 0
+ORDER = (0, 1, 2, 6, 3, 4, 5, 7)
+S_REGROUP = (2, 5, 9)
+TINY = 1e-30
+
+
+def tile_relationembedding_kernel(tc, sbj_vec, obj_vec, W1, b1, W2, b2, label_vecs, out):
+    nc = tc.nc
+    with tc.tile_pool(name="keep", bufs=1) as keep:
+        ident_f = keep.tile([P, P], F32, name="ident_f")
+        make_identity(nc, ident_f[:])
+        ident_b = keep.tile([P, P], BF16, name="ident_b")
+        make_identity(nc, ident_b[:])
+        one = keep.tile([P, 1], F32, name="one")
+        nc.vector.memset(one[:], 1.0)
+        nc.scalar.activation(out=one[:], in_=one[:], func=ACT.Sqrt)
+        biasT = keep.tile([P, 16], F32, name="biasT")
+        labT = keep.tile([P, NO, L], F32, name="labT")
+        embT = keep.tile([P, NO, B], F32, name="embT")
+        w2codes = keep.tile([P, G2, DO], U32, name="w2codes", align_bytes=64)
+        w2scales = keep.tile([P, G2, DO], U8, name="w2scales", align_bytes=64)
+        hcodes = keep.tile([P, G2, B], U32, name="hcodes", align_bytes=64)
+        hscales = keep.tile([P, G2, B], U8, name="hscales", align_bytes=64)
+
+        with tc.tile_pool(name="mx", bufs=1) as mx, tc.tile_pool(name="xraw", bufs=8) as xraw, tc.tile_pool(
+            name="xgrp", bufs=3
+        ) as xgrp, tc.tile_pool(name="wraw", bufs=3) as wraw, tc.tile_pool(name="wgrp", bufs=2) as wgrp, tc.psum_pool(
+            name="pt", bufs=3
+        ) as pt, tc.psum_pool(name="pm", bufs=4) as pm:
+            xcodes = mx.tile([P, G1, B], U32, name="xcodes", align_bytes=64)
+            xscales = mx.tile([P, G1, B], U8, name="xscales", align_bytes=64)
+            w1codes = mx.tile([P, G1, DO], U32, name="w1codes", align_bytes=64)
+            w1scales = mx.tile([P, G1, DO], U8, name="w1scales", align_bytes=64)
+
+            lab_sb = mx.tile([P, DO], BF16, name="lab_sb")
+            nc.scalar.dma_start(out=lab_sb[:], in_=label_vecs)
+            bias_rows = mx.tile([P, P], BF16, name="bias_rows")
+            nc.vector.memset(bias_rows[:], 0.0)
+            nc.scalar.dma_start(out=bias_rows[0:8, :], in_=b1.rearrange("(r c) -> r c", c=P))
+            nc.scalar.dma_start(out=bias_rows[8:16, :], in_=b2.rearrange("(r c) -> r c", c=P))
+
+            xw = {}
+
+            def x_load(h):
+                for s, src in enumerate((sbj_vec, obj_vec)):
+                    for i in range(4):
+                        bb = 4 * h + i
+                        xr = xraw.tile([P, DH], BF16, name="xr", tag="xr")
+                        nc.sync.dma_start(out=xr[:], in_=src[bb * P : (bb + 1) * P, :])
+                        nc.vector.tensor_scalar_max(out=xr[:], in0=xr[:], scalar1=0.0)
+                        xw[(s, bb)] = xr
+
+            def x_pass(h, g):
+                s, gl = divmod(g, 4)
+                grp = xgrp.tile([P, PACK * HB], BF16, name="xg", tag="xg", align_bytes=64)
+                grp_words = grp[:].bitcast(F32).rearrange("p (b u) -> p b u", u=2)
+                for j in range(2):
+                    bank = pt.tile([P, 2, 2 * P], F32, name="xt", tag="xt")
+                    for i2 in range(2):
+                        words = xw[(s, 4 * h + 2 * j + i2)][:].bitcast(F32)
+                        for u in range(2):
+                            c0 = 256 * gl + P * u
+                            nc.tensor.transpose(bank[:, u, i2 * P : (i2 + 1) * P], words[:, c0 : c0 + P], ident_f[:])
+                    nc.scalar.copy(out=grp_words[:, 256 * j : 256 * (j + 1), :], in_=bank[:].rearrange("p u b -> p b u"))
+                cols = slice(h * HB, (h + 1) * HB)
+                nc.vector.quantize_mx(out=xcodes[:, g, cols].bitcast(FP8X4), scales=xscales[:, g, cols], in_=grp[:])
+
+            def regroup_quantise(raw, width, codes, scales, on_scalar):
+                grp = wgrp.tile([P, width, PACK], BF16, name="wg", tag="wg", align_bytes=64)
+                dst = grp[:].rearrange("p (c i) t -> p c t i", i=4)
+                src = raw[:].rearrange("p t (c i) -> p c t i", i=4)
+                if on_scalar:
+                    nc.scalar.copy(out=dst, in_=src)
+                else:
+                    nc.vector.tensor_copy(out=dst, in_=src)
+                nc.vector.quantize_mx(out=codes.bitcast(FP8X4), scales=scales, in_=grp[:].rearrange("p n t -> p (n t)"))
+
+            w1_view = W1.rearrange("(g u q e) n -> g q u (e n)", u=2, q=P, e=2)
+            w2_view = W2.rearrange("(g t p) n -> g p t n", t=PACK, p=P)
+
+            def w1_pass(g):
+                raw = wraw.tile([P, PACK, DO], BF16, name="wr", tag="wr")
+                nc.sync.dma_start(out=raw[:].rearrange("p (u e) n -> p u (e n)", e=2), in_=w1_view[g])
+                regroup_quantise(raw, DO, w1codes[:, g, :], w1scales[:, g, :], g in S_REGROUP)
+
+            def w2_pass(g):
+                raw = wraw.tile([P, PACK, DO], BF16, name="wr", tag="wr")
+                nc.sync.dma_start(out=raw[:], in_=w2_view[g])
+                regroup_quantise(raw, DO, w2codes[:, g, :], w2scales[:, g, :], (G1 + g) in S_REGROUP)
+
+            def hidden(h):
+                cols = slice(h * HB, (h + 1) * HB)
+                for c2 in range(G2):
+                    hr = wraw.tile([P, PACK, HB], BF16, name="hr", tag="wr")
+                    for t in range(PACK):
+                        ob = PACK * c2 + t
+                        ps = pm.tile([P, HB], F32, name="mm", tag="mm")
+                        for g in range(G1):
+                            nc.tensor.matmul_mx(
+                                out=ps[:],
+                                lhsT=w1codes[:, g, ob * P : (ob + 1) * P].bitcast(FP8X4),
+                                lhsT_scale=w1scales[:, g, ob * P : (ob + 1) * P],
+                                rhs=xcodes[:, g, cols].bitcast(FP8X4),
+                                rhs_scale=xscales[:, g, cols],
+                                start=(g == 0),
+                                stop=(g == G1 - 1),
+                            )
+                        nc.scalar.activation(out=hr[:, t, :], in_=ps[:], func=ACT.Relu, bias=biasT[:, ob : ob + 1], scale=1.0)
+                    regroup_quantise(hr, HB, hcodes[:, c2, cols], hscales[:, c2, cols], False)
+
+            def embed(h):
+                cols = slice(h * HB, (h + 1) * HB)
+                for ob in range(NO):
+                    ps = pm.tile([P, HB], F32, name="mm", tag="mm")
+                    for c2 in range(G2):
+                        nc.tensor.matmul_mx(
+                            out=ps[:],
+                            lhsT=w2codes[:, c2, ob * P : (ob + 1) * P].bitcast(FP8X4),
+                            lhsT_scale=w2scales[:, c2, ob * P : (ob + 1) * P],
+                            rhs=hcodes[:, c2, cols].bitcast(FP8X4),
+                            rhs_scale=hscales[:, c2, cols],
+                            start=(c2 == 0),
+                            stop=(c2 == G2 - 1),
+                        )
+                    nc.scalar.activation(
+                        out=embT[:, ob, cols], in_=ps[:], func=ACT.Identity, bias=biasT[:, NO + ob : NO + ob + 1], scale=1.0
+                    )
+
+            x_load(0)
+            for g in range(G1):
+                w1_pass(g)
+                x_pass(0, g)
+
+            tb = pt.tile([P, P], BF16, name="tb", tag="xt")
+            nc.tensor.transpose(tb[:], bias_rows[:], ident_b[:])
+            nc.vector.tensor_copy(out=biasT[:], in_=tb[:, 0:16])
+            tl = pt.tile([P, NO, L], BF16, name="tl", tag="xt")
+            for c in range(NO):
+                nc.tensor.transpose(tl[:, c, :], lab_sb[:, c * P : (c + 1) * P], ident_b[:])
+            nc.vector.tensor_copy(out=labT[:], in_=tl[:])
+
+            x_load(1)
+            for g in range(G2):
+                w2_pass(g)
+            hidden(0)
+            for g in range(G1):
+                x_pass(1, g)
+            embed(0)
+            hidden(1)
+            embed(1)
+
+        seq = [(hf, bb) for hf in range(2) for bb in ORDER]
+        nbank = 8 if KEEP_EVERY == 0 else 7
+        with tc.tile_pool(name="pair", bufs=1) as pair, tc.tile_pool(name="rp", bufs=4) as rp, tc.psum_pool(
+            name="pb", bufs=nbank
+        ) as pb:
+            acc_s = pair.tile([P, 2, NB, L], F32, name="acc_s")
+            stats = pair.tile([P, 2 * 2 * L * 2, 3], F32, name="stats")
+            junk = pair.tile([P, 4 * P], F32, name="junk")
+            rt = {}
+
+            def pass1(l, c):
+                hf, j = divmod(c, 4)
+                if j == 0:
+                    rt[(l, hf)] = rp.tile([P, 4, B], F32, name="r", tag="r")
+                nc.vector.tensor_scalar(
+                    out=rt[(l, hf)][:, j, :],
+                    in0=embT[:, c, :],
+                    scalar1=labT[:, c, l : l + 1],
+                    scalar2=0.0,
+                    op0=ALU.subtract,
+                    op1=ALU.min,
+                )
+
+            with tc.manual_schedule():
+                for c in range(NO):
+                    pass1(0, c)
+                for l in range(L):
+                    for k, (hf, bb) in enumerate(seq):
+                        bank = pb.tile([P, 4 * P], F32, name="bank", tag="bank")
+                        for j in range(4):
+                            nc.tensor.transpose(
+                                bank[:, j * P : (j + 1) * P], rt[(l, hf)][:, j, bb * P : (bb + 1) * P], ident_f[:]
+                            )
+                        if KEEP_EVERY and k % KEEP_EVERY == KEEP_EVERY - 1:
+                            kp = pb.tile([P, HB], F32, name="kp", tag="kp", bufs=1)
+                            nc.tensor.matmul_mx(
+                                out=kp[:],
+                                lhsT=w2codes[:, 0, 0:P].bitcast(FP8X4),
+                                lhsT_scale=w2scales[:, 0, 0:P],
+                                rhs=hcodes[:, 0, 0:HB].bitcast(FP8X4),
+                                rhs_scale=hscales[:, 0, 0:HB],
+                                start=True,
+                                stop=True,
+                            )
+                        if bb >= 6:
+                            n0 = (((bb - 6) * 2 + hf) * L + l) * 2
+                            nc.vector.bn_stats(out=stats[:, n0 : n0 + 2, :].rearrange("p a b -> p (a b)"), in_=bank[:])
+                        else:
+                            nc.scalar.activation(
+                                out=junk[:], in_=bank[:], func=ACT.Square, accum_out=acc_s[:, hf, bb, l : l + 1]
+                            )
+                        if k % 2 == 1 and l + 1 < L:
+                            pass1(l + 1, k // 2)
+
+            res = pair.tile([P, NB, L], F32, name="res")
+            nc.vector.tensor_tensor(out=res[:, 0:6, :], in0=acc_s[:, 0, 0:6, :], in1=acc_s[:, 1, 0:6, :], op=ALU.add)
+            msq = pair.tile([P, 8 * L], F32, name="msq")
+            nc.vector.tensor_tensor(out=msq[:], in0=stats[:, :, 1], in1=stats[:, :, 1], op=ALU.mult)
+            ssq = pair.tile([P, 4 * L, 2], F32, name="ssq")
+            nc.vector.scalar_tensor_tensor(
+                out=ssq[:].rearrange("p n e -> p (n e)"),
+                in0=msq[:],
+                scalar=256.0,
+                in1=stats[:, :, 2],
+                op0=ALU.mult,
+                op1=ALU.add,
+            )
+            se = pair.tile([P, 2, 2, L], F32, name="se")
+            nc.vector.tensor_reduce(out=se[:].rearrange("p i h l -> p (i h l)"), in_=ssq[:], axis=AX.X, op=ALU.add)
+            nc.vector.tensor_tensor(out=res[:, 6:8, :], in0=se[:, :, 0, :], in1=se[:, :, 1, :], op=ALU.add)
+            nc.vector.tensor_scalar_max(out=res[:], in0=res[:], scalar1=TINY)
+            nc.scalar.activation(out=res[:], in_=res[:], func=ACT.Sqrt)
+            nc.vector.tensor_scalar_mul(out=res[:], in0=res[:], scalar1=-1.0)
+            nc.sync.dma_start(out=out.rearrange("(k p) l -> p k l", p=P), in_=res[:])

@@ -23,7 +23,7 @@ NO = DO // P
 
 FLOPS = 2 * B * 2 * DH * DO + 2 * B * DO * DO + 4 * B * L * DO
 
-KEEP_EVERY = 0
+KEEP_EVERY = 4
 ORDER = (0, 1, 2, 6, 3, 4, 5, 7)
 S_REGROUP = (2, 5, 9)
 TINY = 1e-30
@@ -182,7 +182,19 @@ def tile_relationembedding_kernel(tc, sbj_vec, obj_vec, W1, b1, W2, b2, label_ve
             acc_s = pair.tile([P, 2, NB, L], F32, name="acc_s")
             stats = pair.tile([P, 2 * 2 * L * 2, 3], F32, name="stats")
             junk = pair.tile([P, 4 * P], F32, name="junk")
+            kp = pb.tile([P, HB], F32, name="kp", tag="kp", bufs=1)
             rt = {}
+
+            def keeper():
+                nc.tensor.matmul_mx(
+                    out=kp[:],
+                    lhsT=w2codes[:, 0, 0:P].bitcast(FP8X4),
+                    lhsT_scale=w2scales[:, 0, 0:P],
+                    rhs=hcodes[:, 0, 0:HB].bitcast(FP8X4),
+                    rhs_scale=hscales[:, 0, 0:HB],
+                    start=True,
+                    stop=True,
+                )
 
             def pass1(l, c):
                 hf, j = divmod(c, 4)
@@ -200,6 +212,8 @@ def tile_relationembedding_kernel(tc, sbj_vec, obj_vec, W1, b1, W2, b2, label_ve
             with tc.manual_schedule():
                 for c in range(NO):
                     pass1(0, c)
+                for i in range(4):
+                    keeper()
                 for l in range(L):
                     for k, (hf, bb) in enumerate(seq):
                         bank = pb.tile([P, 4 * P], F32, name="bank", tag="bank")
@@ -208,16 +222,7 @@ def tile_relationembedding_kernel(tc, sbj_vec, obj_vec, W1, b1, W2, b2, label_ve
                                 bank[:, j * P : (j + 1) * P], rt[(l, hf)][:, j, bb * P : (bb + 1) * P], ident_f[:]
                             )
                         if KEEP_EVERY and k % KEEP_EVERY == KEEP_EVERY - 1:
-                            kp = pb.tile([P, HB], F32, name="kp", tag="kp", bufs=1)
-                            nc.tensor.matmul_mx(
-                                out=kp[:],
-                                lhsT=w2codes[:, 0, 0:P].bitcast(FP8X4),
-                                lhsT_scale=w2scales[:, 0, 0:P],
-                                rhs=hcodes[:, 0, 0:HB].bitcast(FP8X4),
-                                rhs_scale=hscales[:, 0, 0:HB],
-                                start=True,
-                                stop=True,
-                            )
+                            keeper()
                         if bb >= 6:
                             n0 = (((bb - 6) * 2 + hf) * L + l) * 2
                             nc.vector.bn_stats(out=stats[:, n0 : n0 + 2, :].rearrange("p a b -> p (a b)"), in_=bank[:])

@@ -24,7 +24,8 @@ NO = DO // P
 FLOPS = 2 * B * 2 * DH * DO + 2 * B * DO * DO + 4 * B * L * DO
 
 KEEP_EVERY = 4
-ORDER = (0, 1, 2, 6, 3, 4, 5, 7)
+NV = 1
+ORDER = (0, 1, 2, 7, 3, 4, 5, 6)
 S_REGROUP = (2, 5, 9)
 TINY = 1e-30
 
@@ -180,7 +181,7 @@ def tile_relationembedding_kernel(tc, sbj_vec, obj_vec, W1, b1, W2, b2, label_ve
             name="pb", bufs=nbank
         ) as pb:
             acc_s = pair.tile([P, 2, NB, L], F32, name="acc_s")
-            stats = pair.tile([P, 2 * 2 * L * 2, 3], F32, name="stats")
+            stats = pair.tile([P, NV * 2 * L * 2, 3], F32, name="stats")
             junk = pair.tile([P, 4 * P], F32, name="junk")
             kp = pb.tile([P, HB], F32, name="kp", tag="kp", bufs=1)
             rt = {}
@@ -223,8 +224,8 @@ def tile_relationembedding_kernel(tc, sbj_vec, obj_vec, W1, b1, W2, b2, label_ve
                             )
                         if KEEP_EVERY and k % KEEP_EVERY == KEEP_EVERY - 1:
                             keeper()
-                        if bb >= 6:
-                            n0 = (((bb - 6) * 2 + hf) * L + l) * 2
+                        if bb >= NB - NV:
+                            n0 = (((bb - (NB - NV)) * 2 + hf) * L + l) * 2
                             nc.vector.bn_stats(out=stats[:, n0 : n0 + 2, :].rearrange("p a b -> p (a b)"), in_=bank[:])
                         else:
                             nc.scalar.activation(
@@ -234,10 +235,11 @@ def tile_relationembedding_kernel(tc, sbj_vec, obj_vec, W1, b1, W2, b2, label_ve
                             pass1(l + 1, k // 2)
 
             res = pair.tile([P, NB, L], F32, name="res")
-            nc.vector.tensor_tensor(out=res[:, 0:6, :], in0=acc_s[:, 0, 0:6, :], in1=acc_s[:, 1, 0:6, :], op=ALU.add)
-            msq = pair.tile([P, 8 * L], F32, name="msq")
+            ns = NB - NV
+            nc.vector.tensor_tensor(out=res[:, 0:ns, :], in0=acc_s[:, 0, 0:ns, :], in1=acc_s[:, 1, 0:ns, :], op=ALU.add)
+            msq = pair.tile([P, NV * 4 * L], F32, name="msq")
             nc.vector.tensor_tensor(out=msq[:], in0=stats[:, :, 1], in1=stats[:, :, 1], op=ALU.mult)
-            ssq = pair.tile([P, 4 * L, 2], F32, name="ssq")
+            ssq = pair.tile([P, NV * 2 * L, 2], F32, name="ssq")
             nc.vector.scalar_tensor_tensor(
                 out=ssq[:].rearrange("p n e -> p (n e)"),
                 in0=msq[:],
@@ -246,9 +248,9 @@ def tile_relationembedding_kernel(tc, sbj_vec, obj_vec, W1, b1, W2, b2, label_ve
                 op0=ALU.mult,
                 op1=ALU.add,
             )
-            se = pair.tile([P, 2, 2, L], F32, name="se")
+            se = pair.tile([P, NV, 2, L], F32, name="se")
             nc.vector.tensor_reduce(out=se[:].rearrange("p i h l -> p (i h l)"), in_=ssq[:], axis=AX.X, op=ALU.add)
-            nc.vector.tensor_tensor(out=res[:, 6:8, :], in0=se[:, :, 0, :], in1=se[:, :, 1, :], op=ALU.add)
+            nc.vector.tensor_tensor(out=res[:, ns:NB, :], in0=se[:, :, 0, :], in1=se[:, :, 1, :], op=ALU.add)
             nc.vector.tensor_scalar_max(out=res[:], in0=res[:], scalar1=TINY)
             nc.scalar.activation(out=res[:], in_=res[:], func=ACT.Sqrt)
             nc.vector.tensor_scalar_mul(out=res[:], in0=res[:], scalar1=-1.0)

@@ -24,8 +24,7 @@ NO = DO // P
 FLOPS = 2 * B * 2 * DH * DO + 2 * B * DO * DO + 4 * B * L * DO
 
 KEEP_EVERY = 4
-NV = 1
-ORDER = (0, 1, 2, 7, 3, 4, 5, 6)
+S_COLS = 6 * 1024 + 512
 S_REGROUP = (2, 5, 9)
 TINY = 1e-30
 
@@ -175,16 +174,13 @@ def tile_relationembedding_kernel(tc, sbj_vec, obj_vec, W1, b1, W2, b2, label_ve
             hidden(1)
             embed(1)
 
-        seq = [(hf, bb) for hf in range(2) for bb in ORDER]
-        nbank = 8 if KEEP_EVERY == 0 else 7
         with tc.tile_pool(name="pair", bufs=1) as pair, tc.tile_pool(name="rp", bufs=4) as rp, tc.psum_pool(
-            name="pb", bufs=nbank
+            name="pb", bufs=6
         ) as pb:
-            acc_s = pair.tile([P, 2, NB, L], F32, name="acc_s")
-            stats = pair.tile([P, NV * 2 * L * 2, 3], F32, name="stats")
-            junk = pair.tile([P, 4 * P], F32, name="junk")
+            tot = pair.tile([P, L, NB], F32, name="tot")
             kp = pb.tile([P, HB], F32, name="kp", tag="kp", bufs=1)
             rt = {}
+            banks = {}
 
             def keeper():
                 nc.tensor.matmul_mx(
@@ -198,11 +194,10 @@ def tile_relationembedding_kernel(tc, sbj_vec, obj_vec, W1, b1, W2, b2, label_ve
                 )
 
             def pass1(l, c):
-                hf, j = divmod(c, 4)
-                if j == 0:
-                    rt[(l, hf)] = rp.tile([P, 4, B], F32, name="r", tag="r")
+                if c == 0:
+                    rt[l] = rp.tile([P, NO, B], F32, name="r", tag="r")
                 nc.vector.tensor_scalar(
-                    out=rt[(l, hf)][:, j, :],
+                    out=rt[l][:, c, :],
                     in0=embT[:, c, :],
                     scalar1=labT[:, c, l : l + 1],
                     scalar2=0.0,
@@ -210,48 +205,54 @@ def tile_relationembedding_kernel(tc, sbj_vec, obj_vec, W1, b1, W2, b2, label_ve
                     op1=ALU.min,
                 )
 
+            def squares(l):
+                flat = rt[l][:].rearrange("p c b -> p (c b)")
+                half = S_COLS // 2
+                nc.scalar.activation(out=flat[:, 0:half], in_=flat[:, 0:half], func=ACT.Square)
+                nc.scalar.activation(out=flat[:, half:S_COLS], in_=flat[:, half:S_COLS], func=ACT.Square)
+                nc.vector.tensor_tensor(
+                    out=flat[:, S_COLS : NO * B], in0=flat[:, S_COLS : NO * B], in1=flat[:, S_COLS : NO * B], op=ALU.mult
+                )
+
+            def turn(l):
+                for bb in range(NB):
+                    if bb % 4 == 0:
+                        banks[(l, bb // 4)] = pb.tile([P, 4, P], F32, name="bank", tag="bank")
+                    for c in range(NO):
+                        nc.tensor.matmul(
+                            out=banks[(l, bb // 4)][:, bb % 4, :],
+                            lhsT=rt[l][:, c, bb * P : (bb + 1) * P],
+                            rhs=ident_f[:],
+                            is_transpose=True,
+                            start=(c == 0),
+                            stop=(c == NO - 1),
+                        )
+                    if KEEP_EVERY and bb % 2 == 1:
+                        keeper()
+
+            def drain(l):
+                for q in range(2):
+                    nc.vector.tensor_reduce(out=tot[:, l, 4 * q : 4 * q + 4], in_=banks[(l, q)][:], axis=AX.X, op=ALU.add)
+
             with tc.manual_schedule():
-                for c in range(NO):
-                    pass1(0, c)
                 for i in range(4):
                     keeper()
-                for l in range(L):
-                    for k, (hf, bb) in enumerate(seq):
-                        bank = pb.tile([P, 4 * P], F32, name="bank", tag="bank")
-                        for j in range(4):
-                            nc.tensor.transpose(
-                                bank[:, j * P : (j + 1) * P], rt[(l, hf)][:, j, bb * P : (bb + 1) * P], ident_f[:]
-                            )
-                        if KEEP_EVERY and k % KEEP_EVERY == KEEP_EVERY - 1:
-                            keeper()
-                        if bb >= NB - NV:
-                            n0 = (((bb - (NB - NV)) * 2 + hf) * L + l) * 2
-                            nc.vector.bn_stats(out=stats[:, n0 : n0 + 2, :].rearrange("p a b -> p (a b)"), in_=bank[:])
-                        else:
-                            nc.scalar.activation(
-                                out=junk[:], in_=bank[:], func=ACT.Square, accum_out=acc_s[:, hf, bb, l : l + 1]
-                            )
-                        if k % 2 == 1 and l + 1 < L:
-                            pass1(l + 1, k // 2)
+                for i in range(-2, L + 1):
+                    if i + 2 < L:
+                        for c in range(4):
+                            pass1(i + 2, c)
+                    if i - 1 >= 0:
+                        drain(i - 1)
+                    if 0 <= i + 1 < L:
+                        squares(i + 1)
+                    if i + 2 < L:
+                        for c in range(4, NO):
+                            pass1(i + 2, c)
+                    if 0 <= i < L:
+                        turn(i)
 
             res = pair.tile([P, NB, L], F32, name="res")
-            ns = NB - NV
-            nc.vector.tensor_tensor(out=res[:, 0:ns, :], in0=acc_s[:, 0, 0:ns, :], in1=acc_s[:, 1, 0:ns, :], op=ALU.add)
-            msq = pair.tile([P, NV * 4 * L], F32, name="msq")
-            nc.vector.tensor_tensor(out=msq[:], in0=stats[:, :, 1], in1=stats[:, :, 1], op=ALU.mult)
-            ssq = pair.tile([P, NV * 2 * L, 2], F32, name="ssq")
-            nc.vector.scalar_tensor_tensor(
-                out=ssq[:].rearrange("p n e -> p (n e)"),
-                in0=msq[:],
-                scalar=256.0,
-                in1=stats[:, :, 2],
-                op0=ALU.mult,
-                op1=ALU.add,
-            )
-            se = pair.tile([P, NV, 2, L], F32, name="se")
-            nc.vector.tensor_reduce(out=se[:].rearrange("p i h l -> p (i h l)"), in_=ssq[:], axis=AX.X, op=ALU.add)
-            nc.vector.tensor_tensor(out=res[:, ns:NB, :], in0=se[:, :, 0, :], in1=se[:, :, 1, :], op=ALU.add)
-            nc.vector.tensor_scalar_max(out=res[:], in0=res[:], scalar1=TINY)
-            nc.scalar.activation(out=res[:], in_=res[:], func=ACT.Sqrt)
+            nc.vector.tensor_scalar_max(out=tot[:], in0=tot[:], scalar1=TINY)
+            nc.scalar.activation(out=res[:], in_=tot[:].rearrange("p l k -> p k l"), func=ACT.Sqrt)
             nc.vector.tensor_scalar_mul(out=res[:], in0=res[:], scalar1=-1.0)
             nc.sync.dma_start(out=out.rearrange("(k p) l -> p k l", p=P), in_=res[:])

@@ -26,6 +26,7 @@ FLOPS = 2 * B * 2 * DH * DO + 2 * B * DO * DO + 4 * B * L * DO
 KEEP_EVERY = 4
 S_COLS = 6 * 1024 + 512
 S_REGROUP = (2, 5, 9)
+BURST_EVERY = 8
 TINY = 1e-30
 
 
@@ -215,6 +216,9 @@ def tile_relationembedding_kernel(tc, sbj_vec, obj_vec, W1, b1, W2, b2, label_ve
                 )
 
             def turn(l):
+                if l % BURST_EVERY == 0:
+                    for i in range(3):
+                        keeper()
                 for bb in range(NB):
                     if bb % 4 == 0:
                         banks[(l, bb // 4)] = pb.tile([P, 4, P], F32, name="bank", tag="bank")
@@ -235,8 +239,6 @@ def tile_relationembedding_kernel(tc, sbj_vec, obj_vec, W1, b1, W2, b2, label_ve
                     nc.vector.tensor_reduce(out=tot[:, l, 4 * q : 4 * q + 4], in_=banks[(l, q)][:], axis=AX.X, op=ALU.add)
 
             with tc.manual_schedule():
-                for i in range(4):
-                    keeper()
                 for i in range(-2, L + 1):
                     if i + 2 < L:
                         for c in range(4):

@@ -23,10 +23,10 @@ NO = DO // P
 
 FLOPS = 2 * B * 2 * DH * DO + 2 * B * DO * DO + 4 * B * L * DO
 
-KEEP_EVERY = 4
+KEEP_EVERY = 0
 S_COLS = 6 * 1024 + 512
 S_REGROUP = (2, 5, 9)
-BURST_EVERY = 8
+BURST_EVERY = 1
 TINY = 1e-30
 
 

@@ -26,7 +26,7 @@ FLOPS = 2 * B * 2 * DH * DO + 2 * B * DO * DO + 4 * B * L * DO
 KEEP_EVERY = 0
 S_COLS = 6 * 1024 + 512
 S_REGROUP = (2, 5, 9)
-BURST_EVERY = 1
+BURST_EVERY = 2
 TINY = 1e-30
 
 

@@ -24,7 +24,7 @@ NO = DO // P
 FLOPS = 2 * B * 2 * DH * DO + 2 * B * DO * DO + 4 * B * L * DO
 
 KEEP_EVERY = 0
-S_COLS = 6 * 1024 + 512
+S_COLS = 6 * 1024 + 704
 S_REGROUP = (2, 5, 9)
 BURST_EVERY = 2
 TINY = 1e-30

@@ -25,7 +25,6 @@ FLOPS = 2 * B * 2 * DH * DO + 2 * B * DO * DO + 4 * B * L * DO
 
 KEEP_EVERY = 0
 S_COLS = 6 * 1024 + 704
-S_REGROUP = (2, 5, 9)
 BURST_EVERY = 2
 TINY = 1e-30
 
@@ -48,11 +47,11 @@ def tile_relationembedding_kernel(tc, sbj_vec, obj_vec, W1, b1, W2, b2, label_ve
         hcodes = keep.tile([P, G2, B], U32, name="hcodes", align_bytes=64)
         hscales = keep.tile([P, G2, B], U8, name="hscales", align_bytes=64)
 
-        with tc.tile_pool(name="mx", bufs=1) as mx, tc.tile_pool(name="xraw", bufs=8) as xraw, tc.tile_pool(
-            name="xgrp", bufs=3
-        ) as xgrp, tc.tile_pool(name="wraw", bufs=3) as wraw, tc.tile_pool(name="wgrp", bufs=2) as wgrp, tc.psum_pool(
-            name="pt", bufs=3
-        ) as pt, tc.psum_pool(name="pm", bufs=4) as pm:
+        with tc.tile_pool(name="mx", bufs=1) as mx, tc.tile_pool(name="xraw", bufs=6) as xraw, tc.tile_pool(
+            name="xgrp", bufs=4
+        ) as xgrp, tc.tile_pool(name="wraw", bufs=4) as wraw, tc.tile_pool(name="wgrp", bufs=4) as wgrp, tc.tile_pool(
+            name="hraw", bufs=2
+        ) as hraw:
             xcodes = mx.tile([P, G1, B], U32, name="xcodes", align_bytes=64)
             xscales = mx.tile([P, G1, B], U8, name="xscales", align_bytes=64)
             w1codes = mx.tile([P, G1, DO], U32, name="w1codes", align_bytes=64)
@@ -65,76 +64,117 @@ def tile_relationembedding_kernel(tc, sbj_vec, obj_vec, W1, b1, W2, b2, label_ve
             nc.scalar.dma_start(out=bias_rows[0:8, :], in_=b1.rearrange("(r c) -> r c", c=P))
             nc.scalar.dma_start(out=bias_rows[8:16, :], in_=b2.rearrange("(r c) -> r c", c=P))
 
-            xw = {}
+            x_order = [(s, bb) for h in range(NH) for s in range(2) for bb in range(4 * h, 4 * h + 4)]
+            xr = {}
+            xg = {}
 
-            def x_load(h):
-                for s, src in enumerate((sbj_vec, obj_vec)):
-                    for i in range(4):
-                        bb = 4 * h + i
-                        xr = xraw.tile([P, DH], BF16, name="xr", tag="xr")
-                        nc.sync.dma_start(out=xr[:], in_=src[bb * P : (bb + 1) * P, :])
-                        nc.vector.tensor_scalar_max(out=xr[:], in0=xr[:], scalar1=0.0)
-                        xw[(s, bb)] = xr
+            def x_load(i):
+                s, bb = x_order[i]
+                xr[i] = xraw.tile([P, DH], BF16, name="xr", tag="xr")
+                nc.sync.dma_start(out=xr[i][:], in_=(sbj_vec, obj_vec)[s][bb * P : (bb + 1) * P, :])
+                nc.vector.tensor_scalar_max(out=xr[i][:], in0=xr[i][:], scalar1=0.0)
 
-            def x_pass(h, g):
-                s, gl = divmod(g, 4)
-                grp = xgrp.tile([P, PACK * HB], BF16, name="xg", tag="xg", align_bytes=64)
-                grp_words = grp[:].bitcast(F32).rearrange("p (b u) -> p b u", u=2)
+            def x_turn(pt, i):
+                words = xr[i][:].bitcast(F32)
                 for j in range(2):
-                    bank = pt.tile([P, 2, 2 * P], F32, name="xt", tag="xt")
-                    for i2 in range(2):
-                        words = xw[(s, 4 * h + 2 * j + i2)][:].bitcast(F32)
+                    bank = pt.tile([P, 2, 2, P], F32, name="xt", tag="xt")
+                    for g2 in range(2):
                         for u in range(2):
-                            c0 = 256 * gl + P * u
-                            nc.tensor.transpose(bank[:, u, i2 * P : (i2 + 1) * P], words[:, c0 : c0 + P], ident_f[:])
-                    nc.scalar.copy(out=grp_words[:, 256 * j : 256 * (j + 1), :], in_=bank[:].rearrange("p u b -> p b u"))
-                cols = slice(h * HB, (h + 1) * HB)
-                nc.vector.quantize_mx(out=xcodes[:, g, cols].bitcast(FP8X4), scales=xscales[:, g, cols], in_=grp[:])
+                            c0 = 256 * (2 * j + g2) + P * u
+                            nc.tensor.transpose(bank[:, g2, u, :], words[:, c0 : c0 + P], ident_f[:])
+                    xg[(i, j)] = xgrp.tile([P, 2, PACK * P], BF16, name="xg", tag="xg", align_bytes=64)
+                    nc.scalar.copy(
+                        out=xg[(i, j)][:].bitcast(F32).rearrange("p g (b u) -> p g b u", u=2),
+                        in_=bank[:].rearrange("p g u b -> p g b u"),
+                    )
 
-            def regroup_quantise(raw, width, codes, scales, on_scalar):
-                grp = wgrp.tile([P, width, PACK], BF16, name="wg", tag="wg", align_bytes=64)
-                dst = grp[:].rearrange("p (c i) t -> p c t i", i=4)
-                src = raw[:].rearrange("p t (c i) -> p c t i", i=4)
+            def x_quant(i):
+                s, bb = x_order[i]
+                cols = slice(bb * P, (bb + 1) * P)
+                for j in range(2):
+                    for g2 in range(2):
+                        g = 4 * s + 2 * j + g2
+                        nc.vector.quantize_mx(
+                            out=xcodes[:, g, cols].bitcast(FP8X4), scales=xscales[:, g, cols], in_=xg[(i, j)][:, g2, :]
+                        )
+
+            with tc.psum_pool(name="pt", bufs=4) as pt:
+                for i in range(len(x_order) + 1):
+                    if i < len(x_order):
+                        x_load(i)
+                        x_turn(pt, i)
+                    if i >= 1:
+                        x_quant(i - 1)
+                tb = pt.tile([P, P], BF16, name="tb", tag="xt")
+                nc.tensor.transpose(tb[:], bias_rows[:], ident_b[:])
+                nc.vector.tensor_copy(out=biasT[:], in_=tb[:, 0:16])
+                tl = pt.tile([P, NO, L], BF16, name="tl", tag="xt")
+                for c in range(NO):
+                    nc.tensor.transpose(tl[:, c, :], lab_sb[:, c * P : (c + 1) * P], ident_b[:])
+                nc.vector.tensor_copy(out=labT[:], in_=tl[:])
+
+            w1_view = W1.rearrange("(g u q e) n -> g q u (e n)", u=2, q=P, e=2)
+            w2_view = W2.rearrange("(g t p) n -> g p t n", t=PACK, p=P)
+            wr = {}
+            wg = {}
+
+            def w_load(g):
+                wr[g] = wraw.tile([P, PACK, DO], BF16, name="wr", tag="wr")
+                if g < G1:
+                    nc.sync.dma_start(out=wr[g][:].rearrange("p (u e) n -> p u (e n)", e=2), in_=w1_view[g])
+                else:
+                    nc.sync.dma_start(out=wr[g][:], in_=w2_view[g - G1])
+
+            def regroup(raw_view, key, on_scalar):
+                wg[key] = wgrp.tile([P, HB, PACK], BF16, name="wg", tag="wg", align_bytes=64)
+                dst = wg[key][:].rearrange("p (c i) t -> p c t i", i=4)
+                src = raw_view.rearrange("p t (c i) -> p c t i", i=4)
                 if on_scalar:
                     nc.scalar.copy(out=dst, in_=src)
                 else:
                     nc.vector.tensor_copy(out=dst, in_=src)
-                nc.vector.quantize_mx(out=codes.bitcast(FP8X4), scales=scales, in_=grp[:].rearrange("p n t -> p (n t)"))
 
-            w1_view = W1.rearrange("(g u q e) n -> g q u (e n)", u=2, q=P, e=2)
-            w2_view = W2.rearrange("(g t p) n -> g p t n", t=PACK, p=P)
+            def quantise(key, codes, scales):
+                nc.vector.quantize_mx(out=codes.bitcast(FP8X4), scales=scales, in_=wg[key][:].rearrange("p n t -> p (n t)"))
 
-            def w1_pass(g):
-                raw = wraw.tile([P, PACK, DO], BF16, name="wr", tag="wr")
-                nc.sync.dma_start(out=raw[:].rearrange("p (u e) n -> p u (e n)", e=2), in_=w1_view[g])
-                regroup_quantise(raw, DO, w1codes[:, g, :], w1scales[:, g, :], g in S_REGROUP)
+            def w_regroup(g):
+                for nh in range(2):
+                    regroup(wr[g][:, :, nh * HB : (nh + 1) * HB], (g, nh), nh == 1)
 
-            def w2_pass(g):
-                raw = wraw.tile([P, PACK, DO], BF16, name="wr", tag="wr")
-                nc.sync.dma_start(out=raw[:], in_=w2_view[g])
-                regroup_quantise(raw, DO, w2codes[:, g, :], w2scales[:, g, :], (G1 + g) in S_REGROUP)
+            def w_quant(g):
+                for nh in range(2):
+                    cols = slice(nh * HB, (nh + 1) * HB)
+                    if g < G1:
+                        quantise((g, nh), w1codes[:, g, cols], w1scales[:, g, cols])
+                    else:
+                        quantise((g, nh), w2codes[:, g - G1, cols], w2scales[:, g - G1, cols])
 
-            def hidden(h):
+            def hidden_pass(ps, h, ob, g):
                 cols = slice(h * HB, (h + 1) * HB)
-                for c2 in range(G2):
-                    hr = wraw.tile([P, PACK, HB], BF16, name="hr", tag="wr")
-                    for t in range(PACK):
-                        ob = PACK * c2 + t
-                        ps = pm.tile([P, HB], F32, name="mm", tag="mm")
-                        for g in range(G1):
-                            nc.tensor.matmul_mx(
-                                out=ps[:],
-                                lhsT=w1codes[:, g, ob * P : (ob + 1) * P].bitcast(FP8X4),
-                                lhsT_scale=w1scales[:, g, ob * P : (ob + 1) * P],
-                                rhs=xcodes[:, g, cols].bitcast(FP8X4),
-                                rhs_scale=xscales[:, g, cols],
-                                start=(g == 0),
-                                stop=(g == G1 - 1),
-                            )
-                        nc.scalar.activation(out=hr[:, t, :], in_=ps[:], func=ACT.Relu, bias=biasT[:, ob : ob + 1], scale=1.0)
-                    regroup_quantise(hr, HB, hcodes[:, c2, cols], hscales[:, c2, cols], False)
+                nc.tensor.matmul_mx(
+                    out=ps[:],
+                    lhsT=w1codes[:, g, ob * P : (ob + 1) * P].bitcast(FP8X4),
+                    lhsT_scale=w1scales[:, g, ob * P : (ob + 1) * P],
+                    rhs=xcodes[:, g, cols].bitcast(FP8X4),
+                    rhs_scale=xscales[:, g, cols],
+                    start=(g == 0),
+                    stop=(g == G1 - 1),
+                )
 
-            def embed(h):
+            hr = {}
+
+            def hidden_out(ps, h, ob):
+                c2, t = divmod(ob, PACK)
+                if t == 0:
+                    hr[(h, c2)] = hraw.tile([P, PACK, HB], BF16, name="hr", tag="hr")
+                nc.scalar.activation(out=hr[(h, c2)][:, t, :], in_=ps[:], func=ACT.Relu, bias=biasT[:, ob : ob + 1], scale=1.0)
+
+            def hidden_quant(h, c2):
+                cols = slice(h * HB, (h + 1) * HB)
+                regroup(hr[(h, c2)][:], ("h", h, c2), False)
+                quantise(("h", h, c2), hcodes[:, c2, cols], hscales[:, c2, cols])
+
+            def embed(pm, h):
                 cols = slice(h * HB, (h + 1) * HB)
                 for ob in range(NO):
                     ps = pm.tile([P, HB], F32, name="mm", tag="mm")
@@ -152,28 +192,35 @@ def tile_relationembedding_kernel(tc, sbj_vec, obj_vec, W1, b1, W2, b2, label_ve
                         out=embT[:, ob, cols], in_=ps[:], func=ACT.Identity, bias=biasT[:, NO + ob : NO + ob + 1], scale=1.0
                     )
 
-            x_load(0)
-            for g in range(G1):
-                w1_pass(g)
-                x_pass(0, g)
-
-            tb = pt.tile([P, P], BF16, name="tb", tag="xt")
-            nc.tensor.transpose(tb[:], bias_rows[:], ident_b[:])
-            nc.vector.tensor_copy(out=biasT[:], in_=tb[:, 0:16])
-            tl = pt.tile([P, NO, L], BF16, name="tl", tag="xt")
-            for c in range(NO):
-                nc.tensor.transpose(tl[:, c, :], lab_sb[:, c * P : (c + 1) * P], ident_b[:])
-            nc.vector.tensor_copy(out=labT[:], in_=tl[:])
-
-            x_load(1)
-            for g in range(G2):
-                w2_pass(g)
-            hidden(0)
-            for g in range(G1):
-                x_pass(1, g)
-            embed(0)
-            hidden(1)
-            embed(1)
+            with tc.psum_pool(name="pm", bufs=8) as pm:
+                acc = [pm.tile([P, HB], F32, name="mm", tag="mm") for ob in range(NO)]
+                for g in range(G1 + 2):
+                    if g < G1:
+                        w_load(g)
+                        w_regroup(g)
+                    if 1 <= g <= G1:
+                        w_quant(g - 1)
+                    if g >= 2:
+                        for ob in range(NO):
+                            hidden_pass(acc[ob], 0, ob, g - 2)
+                for g in range(G1, G1 + G2):
+                    w_load(g)
+                for ob in range(NO):
+                    hidden_out(acc[ob], 0, ob)
+                    if ob % PACK == PACK - 1:
+                        hidden_quant(0, ob // PACK)
+                for g in range(G1, G1 + G2):
+                    w_regroup(g)
+                    w_quant(g)
+                for ob in range(NO):
+                    ps = pm.tile([P, HB], F32, name="mm", tag="mm")
+                    for g in range(G1):
+                        hidden_pass(ps, 1, ob, g)
+                    hidden_out(ps, 1, ob)
+                    if ob % PACK == PACK - 1:
+                        hidden_quant(1, ob // PACK)
+                embed(pm, 0)
+                embed(pm, 1)
 
         with tc.tile_pool(name="pair", bufs=1) as pair, tc.tile_pool(name="rp", bufs=4) as rp, tc.psum_pool(
             name="pb", bufs=6
@@ -215,6 +262,14 @@ def tile_relationembedding_kernel(tc, sbj_vec, obj_vec, W1, b1, W2, b2, label_ve
                     out=flat[:, S_COLS : NO * B], in0=flat[:, S_COLS : NO * B], in1=flat[:, S_COLS : NO * B], op=ALU.mult
                 )
 
+            def squares_last(l):
+                for q in range(4):
+                    piece = rt[l][:, :, 2 * q * P : 2 * (q + 1) * P]
+                    if q % 2 == 0:
+                        nc.scalar.activation(out=piece, in_=piece, func=ACT.Square)
+                    else:
+                        nc.vector.tensor_tensor(out=piece, in0=piece, in1=piece, op=ALU.mult)
+
             def turn(l):
                 if l % BURST_EVERY == 0:
                     for i in range(3):
@@ -245,8 +300,10 @@ def tile_relationembedding_kernel(tc, sbj_vec, obj_vec, W1, b1, W2, b2, label_ve
                             pass1(i + 2, c)
                     if i - 1 >= 0:
                         drain(i - 1)
-                    if 0 <= i + 1 < L:
+                    if 0 <= i + 1 < L - 1:
                         squares(i + 1)
+                    if i + 1 == L - 1:
+                        squares_last(i + 1)
                     if i + 2 < L:
                         for c in range(4, NO):
                             pass1(i + 2, c)

@@ -24,8 +24,10 @@ NO = DO // P
 FLOPS = 2 * B * 2 * DH * DO + 2 * B * DO * DO + 4 * B * L * DO
 
 KEEP_EVERY = 0
-S_COLS = 6 * 1024 + 704
-BURST_EVERY = 2
+S_COLS = 6 * 1024 + 384
+G_COLS = 512
+G_FROM = 8 * 1024 - G_COLS
+BURST_EVERY = 4
 TINY = 1e-30
 
 
@@ -222,12 +224,13 @@ def tile_relationembedding_kernel(tc, sbj_vec, obj_vec, W1, b1, W2, b2, label_ve
                 embed(pm, 0)
                 embed(pm, 1)
 
-        with tc.tile_pool(name="pair", bufs=1) as pair, tc.tile_pool(name="rp", bufs=4) as rp, tc.psum_pool(
-            name="pb", bufs=6
-        ) as pb:
+        with tc.tile_pool(name="pair", bufs=1) as pair, tc.tile_pool(name="rp", bufs=4) as rp, tc.tile_pool(
+            name="gq", bufs=4
+        ) as gq, tc.psum_pool(name="pb", bufs=6) as pb:
             tot = pair.tile([P, L, NB], F32, name="tot")
             kp = pb.tile([P, HB], F32, name="kp", tag="kp", bufs=1)
             rt = {}
+            gs = {}
             banks = {}
 
             def keeper():
@@ -259,8 +262,16 @@ def tile_relationembedding_kernel(tc, sbj_vec, obj_vec, W1, b1, W2, b2, label_ve
                 nc.scalar.activation(out=flat[:, 0:half], in_=flat[:, 0:half], func=ACT.Square)
                 nc.scalar.activation(out=flat[:, half:S_COLS], in_=flat[:, half:S_COLS], func=ACT.Square)
                 nc.vector.tensor_tensor(
-                    out=flat[:, S_COLS : NO * B], in0=flat[:, S_COLS : NO * B], in1=flat[:, S_COLS : NO * B], op=ALU.mult
+                    out=flat[:, S_COLS:G_FROM], in0=flat[:, S_COLS:G_FROM], in1=flat[:, S_COLS:G_FROM], op=ALU.mult
                 )
+
+            def gate(l):
+                gs[l] = gq.tile([P, G_COLS], F32, name="gs", tag="gs")
+                nc.vector.memset(gs[l][:, 0:1], 0.0)
+
+            def squares_g(l):
+                flat = rt[l][:].rearrange("p c b -> p (c b)")
+                nc.gpsimd.tensor_tensor(out=gs[l][:], in0=flat[:, G_FROM : NO * B], in1=flat[:, G_FROM : NO * B], op=ALU.mult)
 
             def squares_last(l):
                 for q in range(4):
@@ -278,9 +289,12 @@ def tile_relationembedding_kernel(tc, sbj_vec, obj_vec, W1, b1, W2, b2, label_ve
                     if bb % 4 == 0:
                         banks[(l, bb // 4)] = pb.tile([P, 4, P], F32, name="bank", tag="bank")
                     for c in range(NO):
+                        block = rt[l][:, c, bb * P : (bb + 1) * P]
+                        if l in gs and c * B + bb * P >= G_FROM:
+                            block = gs[l][:, c * B + bb * P - G_FROM : c * B + (bb + 1) * P - G_FROM]
                         nc.tensor.matmul(
                             out=banks[(l, bb // 4)][:, bb % 4, :],
-                            lhsT=rt[l][:, c, bb * P : (bb + 1) * P],
+                            lhsT=block,
                             rhs=ident_f[:],
                             is_transpose=True,
                             start=(c == 0),
@@ -296,11 +310,16 @@ def tile_relationembedding_kernel(tc, sbj_vec, obj_vec, W1, b1, W2, b2, label_ve
             with tc.manual_schedule():
                 for i in range(-2, L + 1):
                     if i + 2 < L:
-                        for c in range(4):
+                        for c in range(3):
                             pass1(i + 2, c)
+                    if 0 <= i + 1 < L - 1:
+                        gate(i + 1)
+                    if i + 2 < L:
+                        pass1(i + 2, 3)
                     if i - 1 >= 0:
                         drain(i - 1)
                     if 0 <= i + 1 < L - 1:
+                        squares_g(i + 1)
                         squares(i + 1)
                     if i + 1 == L - 1:
                         squares_last(i + 1)

@@ -23,7 +23,6 @@ NO = DO // P
 
 FLOPS = 2 * B * 2 * DH * DO + 2 * B * DO * DO + 4 * B * L * DO
 
-KEEP_EVERY = 0
 S_COLS = 6 * 1024 + 384
 G_COLS = 512
 G_FROM = 8 * 1024 - G_COLS
@@ -274,9 +273,9 @@ def tile_relationembedding_kernel(tc, sbj_vec, obj_vec, W1, b1, W2, b2, label_ve
                 nc.gpsimd.tensor_tensor(out=gs[l][:], in0=flat[:, G_FROM : NO * B], in1=flat[:, G_FROM : NO * B], op=ALU.mult)
 
             def squares_last(l):
-                for q in range(4):
+                for q in (0, 2, 1, 3):
                     piece = rt[l][:, :, 2 * q * P : 2 * (q + 1) * P]
-                    if q % 2 == 0:
+                    if q < 2:
                         nc.scalar.activation(out=piece, in_=piece, func=ACT.Square)
                     else:
                         nc.vector.tensor_tensor(out=piece, in0=piece, in1=piece, op=ALU.mult)
@@ -285,23 +284,23 @@ def tile_relationembedding_kernel(tc, sbj_vec, obj_vec, W1, b1, W2, b2, label_ve
                 if l % BURST_EVERY == 0:
                     for i in range(3):
                         keeper()
-                for bb in range(NB):
-                    if bb % 4 == 0:
-                        banks[(l, bb // 4)] = pb.tile([P, 4, P], F32, name="bank", tag="bank")
+                for q in range(2):
+                    banks[(l, q)] = pb.tile([P, 4, P], F32, name="bank", tag="bank")
+                for k in range(4):
                     for c in range(NO):
-                        block = rt[l][:, c, bb * P : (bb + 1) * P]
-                        if l in gs and c * B + bb * P >= G_FROM:
-                            block = gs[l][:, c * B + bb * P - G_FROM : c * B + (bb + 1) * P - G_FROM]
-                        nc.tensor.matmul(
-                            out=banks[(l, bb // 4)][:, bb % 4, :],
-                            lhsT=block,
-                            rhs=ident_f[:],
-                            is_transpose=True,
-                            start=(c == 0),
-                            stop=(c == NO - 1),
-                        )
-                    if KEEP_EVERY and bb % 2 == 1:
-                        keeper()
+                        for q in range(2):
+                            bb = 4 * q + k
+                            block = rt[l][:, c, bb * P : (bb + 1) * P]
+                            if l in gs and c * B + bb * P >= G_FROM:
+                                block = gs[l][:, c * B + bb * P - G_FROM : c * B + (bb + 1) * P - G_FROM]
+                            nc.tensor.matmul(
+                                out=banks[(l, q)][:, k, :],
+                                lhsT=block,
+                                rhs=ident_f[:],
+                                is_transpose=True,
+                                start=(c == 0),
+                                stop=(c == NO - 1),
+                            )
 
             def drain(l):
                 for q in range(2):

@@ -23,9 +23,8 @@ NO = DO // P
 
 FLOPS = 2 * B * 2 * DH * DO + 2 * B * DO * DO + 4 * B * L * DO
 
-S_COLS = 6 * 1024 + 384
-G_COLS = 512
-G_FROM = 8 * 1024 - G_COLS
+V_B = 144
+G_B = 64
 BURST_EVERY = 4
 TINY = 1e-30
 
@@ -224,12 +223,12 @@ def tile_relationembedding_kernel(tc, sbj_vec, obj_vec, W1, b1, W2, b2, label_ve
                 embed(pm, 1)
 
         with tc.tile_pool(name="pair", bufs=1) as pair, tc.tile_pool(name="rp", bufs=4) as rp, tc.tile_pool(
-            name="gq", bufs=4
-        ) as gq, tc.psum_pool(name="pb", bufs=6) as pb:
+            name="sp", bufs=4
+        ) as sp, tc.psum_pool(name="pb", bufs=6) as pb:
             tot = pair.tile([P, L, NB], F32, name="tot")
             kp = pb.tile([P, HB], F32, name="kp", tag="kp", bufs=1)
             rt = {}
-            gs = {}
+            side = {}
             banks = {}
 
             def keeper():
@@ -255,30 +254,24 @@ def tile_relationembedding_kernel(tc, sbj_vec, obj_vec, W1, b1, W2, b2, label_ve
                     op1=ALU.min,
                 )
 
-            def squares(l):
-                flat = rt[l][:].rearrange("p c b -> p (c b)")
-                half = S_COLS // 2
-                nc.scalar.activation(out=flat[:, 0:half], in_=flat[:, 0:half], func=ACT.Square)
-                nc.scalar.activation(out=flat[:, half:S_COLS], in_=flat[:, half:S_COLS], func=ACT.Square)
-                nc.vector.tensor_tensor(
-                    out=flat[:, S_COLS:G_FROM], in0=flat[:, S_COLS:G_FROM], in1=flat[:, S_COLS:G_FROM], op=ALU.mult
-                )
+            def squares_v(l):
+                piece = rt[l][:, :, 0:V_B]
+                nc.vector.tensor_tensor(out=piece, in0=piece, in1=piece, op=ALU.mult)
 
             def gate(l):
-                gs[l] = gq.tile([P, G_COLS], F32, name="gs", tag="gs")
-                nc.vector.memset(gs[l][:, 0:1], 0.0)
+                side[l] = sp.tile([P, NO, P], F32, name="side", tag="side")
+                nc.vector.memset(side[l][:, 0, P - G_B : P - G_B + 1], 0.0)
 
             def squares_g(l):
-                flat = rt[l][:].rearrange("p c b -> p (c b)")
-                nc.gpsimd.tensor_tensor(out=gs[l][:], in0=flat[:, G_FROM : NO * B], in1=flat[:, G_FROM : NO * B], op=ALU.mult)
+                nc.gpsimd.tensor_tensor(
+                    out=side[l][:, :, P - G_B : P], in0=rt[l][:, :, B - G_B : B], in1=rt[l][:, :, B - G_B : B], op=ALU.mult
+                )
 
-            def squares_last(l):
-                for q in (0, 2, 1, 3):
-                    piece = rt[l][:, :, 2 * q * P : 2 * (q + 1) * P]
-                    if q < 2:
-                        nc.scalar.activation(out=piece, in_=piece, func=ACT.Square)
-                    else:
-                        nc.vector.tensor_tensor(out=piece, in0=piece, in1=piece, op=ALU.mult)
+            def squares_s(l):
+                for b0, b1 in ((V_B, 2 * P), (2 * P, 4 * P), (4 * P, 6 * P), (6 * P, 7 * P)):
+                    piece = rt[l][:, :, b0:b1]
+                    nc.scalar.activation(out=piece, in_=piece, func=ACT.Square)
+                nc.scalar.activation(out=side[l][:, :, 0 : P - G_B], in_=rt[l][:, :, 7 * P : B - G_B], func=ACT.Square)
 
             def turn(l):
                 if l % BURST_EVERY == 0:
@@ -289,10 +282,10 @@ def tile_relationembedding_kernel(tc, sbj_vec, obj_vec, W1, b1, W2, b2, label_ve
                 for k in range(4):
                     for c in range(NO):
                         for q in range(2):
-                            bb = 4 * q + k
+                            bb = 2 * k + q
                             block = rt[l][:, c, bb * P : (bb + 1) * P]
-                            if l in gs and c * B + bb * P >= G_FROM:
-                                block = gs[l][:, c * B + bb * P - G_FROM : c * B + (bb + 1) * P - G_FROM]
+                            if bb == NB - 1:
+                                block = side[l][:, c, :]
                             nc.tensor.matmul(
                                 out=banks[(l, q)][:, k, :],
                                 lhsT=block,
@@ -304,29 +297,29 @@ def tile_relationembedding_kernel(tc, sbj_vec, obj_vec, W1, b1, W2, b2, label_ve
 
             def drain(l):
                 for q in range(2):
-                    nc.vector.tensor_reduce(out=tot[:, l, 4 * q : 4 * q + 4], in_=banks[(l, q)][:], axis=AX.X, op=ALU.add)
+                    nc.vector.tensor_reduce(out=tot[:, l, q:NB:2], in_=banks[(l, q)][:], axis=AX.X, op=ALU.add)
 
             with tc.manual_schedule():
                 for i in range(-2, L + 1):
+                    if 0 <= i + 1 < L:
+                        squares_v(i + 1)
                     if i + 2 < L:
                         for c in range(3):
                             pass1(i + 2, c)
-                    if 0 <= i + 1 < L - 1:
+                    if 0 <= i + 1 < L:
                         gate(i + 1)
                     if i + 2 < L:
                         pass1(i + 2, 3)
                     if i - 1 >= 0:
                         drain(i - 1)
-                    if 0 <= i + 1 < L - 1:
+                    if 0 <= i + 1 < L:
                         squares_g(i + 1)
-                        squares(i + 1)
-                    if i + 1 == L - 1:
-                        squares_last(i + 1)
+                        squares_s(i + 1)
                     if i + 2 < L:
                         for c in range(4, NO):
                             pass1(i + 2, c)
-                    if 0 <= i < L:
-                        turn(i)
+                    if 0 <= i + 1 < L:
+                        turn(i + 1)
 
             res = pair.tile([P, NB, L], F32, name="res")
             nc.vector.tensor_scalar_max(out=tot[:], in0=tot[:], scalar1=TINY)

@@ -24,9 +24,9 @@ NO = DO // P
 FLOPS = 2 * B * 2 * DH * DO + 2 * B * DO * DO + 4 * B * L * DO
 
 V_B = 144
-G_B = 64
 BURST_EVERY = 4
 TINY = 1e-30
+LATE = 16
 
 
 def tile_relationembedding_kernel(tc, sbj_vec, obj_vec, W1, b1, W2, b2, label_vecs, out):
@@ -223,12 +223,12 @@ def tile_relationembedding_kernel(tc, sbj_vec, obj_vec, W1, b1, W2, b2, label_ve
                 embed(pm, 1)
 
         with tc.tile_pool(name="pair", bufs=1) as pair, tc.tile_pool(name="rp", bufs=4) as rp, tc.tile_pool(
-            name="sp", bufs=4
-        ) as sp, tc.psum_pool(name="pb", bufs=6) as pb:
+            name="gq", bufs=4
+        ) as gq, tc.psum_pool(name="pb", bufs=6) as pb:
             tot = pair.tile([P, L, NB], F32, name="tot")
             kp = pb.tile([P, HB], F32, name="kp", tag="kp", bufs=1)
             rt = {}
-            side = {}
+            gs = {}
             banks = {}
 
             def keeper():
@@ -259,19 +259,16 @@ def tile_relationembedding_kernel(tc, sbj_vec, obj_vec, W1, b1, W2, b2, label_ve
                 nc.vector.tensor_tensor(out=piece, in0=piece, in1=piece, op=ALU.mult)
 
             def gate(l):
-                side[l] = sp.tile([P, NO, P], F32, name="side", tag="side")
-                nc.vector.memset(side[l][:, 0, P - G_B : P - G_B + 1], 0.0)
+                gs[l] = gq.tile([P, HB], F32, name="gs", tag="gs")
+                nc.vector.memset(gs[l][:, 0:1], 0.0)
 
             def squares_g(l):
-                nc.gpsimd.tensor_tensor(
-                    out=side[l][:, :, P - G_B : P], in0=rt[l][:, :, B - G_B : B], in1=rt[l][:, :, B - G_B : B], op=ALU.mult
-                )
+                nc.gpsimd.tensor_tensor(out=gs[l][:], in0=rt[l][:, NO - 1, HB:B], in1=rt[l][:, NO - 1, HB:B], op=ALU.mult)
 
             def squares_s(l):
-                for b0, b1 in ((V_B, 2 * P), (2 * P, 4 * P), (4 * P, 6 * P), (6 * P, 7 * P)):
-                    piece = rt[l][:, :, b0:b1]
+                for b0, b1, blocks in ((V_B, 2 * P, NO), (2 * P, 4 * P, NO), (4 * P, 6 * P, NO - 1), (6 * P, 8 * P, NO - 1)):
+                    piece = rt[l][:, 0:blocks, b0:b1]
                     nc.scalar.activation(out=piece, in_=piece, func=ACT.Square)
-                nc.scalar.activation(out=side[l][:, :, 0 : P - G_B], in_=rt[l][:, :, 7 * P : B - G_B], func=ACT.Square)
 
             def turn(l):
                 if l % BURST_EVERY == 0:
@@ -284,8 +281,8 @@ def tile_relationembedding_kernel(tc, sbj_vec, obj_vec, W1, b1, W2, b2, label_ve
                         for q in range(2):
                             bb = 2 * k + q
                             block = rt[l][:, c, bb * P : (bb + 1) * P]
-                            if bb == NB - 1:
-                                block = side[l][:, c, :]
+                            if c == NO - 1 and bb * P >= HB:
+                                block = gs[l][:, bb * P - HB : (bb + 1) * P - HB]
                             nc.tensor.matmul(
                                 out=banks[(l, q)][:, k, :],
                                 lhsT=block,
@@ -298,6 +295,14 @@ def tile_relationembedding_kernel(tc, sbj_vec, obj_vec, W1, b1, W2, b2, label_ve
             def drain(l):
                 for q in range(2):
                     nc.vector.tensor_reduce(out=tot[:, l, q:NB:2], in_=banks[(l, q)][:], axis=AX.X, op=ALU.add)
+
+            res = pair.tile([P, NB, L], F32, name="res")
+
+            def finish(l0, l1):
+                nc.vector.tensor_scalar_max(out=tot[:, l0:l1, :], in0=tot[:, l0:l1, :], scalar1=TINY)
+                nc.scalar.activation(out=res[:, :, l0:l1], in_=tot[:, l0:l1, :].rearrange("p l k -> p k l"), func=ACT.Sqrt)
+                nc.vector.tensor_scalar_mul(out=res[:, :, l0:l1], in0=res[:, :, l0:l1], scalar1=-1.0)
+                nc.sync.dma_start(out=out.rearrange("(k p) l -> p k l", p=P)[:, :, l0:l1], in_=res[:, :, l0:l1])
 
             with tc.manual_schedule():
                 for i in range(-2, L + 1):
@@ -320,9 +325,7 @@ def tile_relationembedding_kernel(tc, sbj_vec, obj_vec, W1, b1, W2, b2, label_ve
                             pass1(i + 2, c)
                     if 0 <= i + 1 < L:
                         turn(i + 1)
+                    if i == L - 2:
+                        finish(0, L - LATE)
 
-            res = pair.tile([P, NB, L], F32, name="res")
-            nc.vector.tensor_scalar_max(out=tot[:], in0=tot[:], scalar1=TINY)
-            nc.scalar.activation(out=res[:], in_=tot[:].rearrange("p l k -> p k l"), func=ACT.Sqrt)
-            nc.vector.tensor_scalar_mul(out=res[:], in0=res[:], scalar1=-1.0)
-            nc.sync.dma_start(out=out.rearrange("(k p) l -> p k l", p=P), in_=res[:])
+            finish(L - LATE, L)

@@ -23,7 +23,7 @@ NO = DO // P
 
 FLOPS = 2 * B * 2 * DH * DO + 2 * B * DO * DO + 4 * B * L * DO
 
-V_B = 144
+V_FROM = 856
 BURST_EVERY = 4
 TINY = 1e-30
 LATE = 16
@@ -255,7 +255,7 @@ def tile_relationembedding_kernel(tc, sbj_vec, obj_vec, W1, b1, W2, b2, label_ve
                 )
 
             def squares_v(l):
-                piece = rt[l][:, :, 0:V_B]
+                piece = rt[l][:, 0 : NO - 1, V_FROM:B]
                 nc.vector.tensor_tensor(out=piece, in0=piece, in1=piece, op=ALU.mult)
 
             def gate(l):
@@ -266,7 +266,7 @@ def tile_relationembedding_kernel(tc, sbj_vec, obj_vec, W1, b1, W2, b2, label_ve
                 nc.gpsimd.tensor_tensor(out=gs[l][:], in0=rt[l][:, NO - 1, HB:B], in1=rt[l][:, NO - 1, HB:B], op=ALU.mult)
 
             def squares_s(l):
-                for b0, b1, blocks in ((V_B, 2 * P, NO), (2 * P, 4 * P, NO), (4 * P, 6 * P, NO - 1), (6 * P, 8 * P, NO - 1)):
+                for b0, b1, blocks in ((0, 2 * P, NO), (2 * P, 4 * P, NO), (4 * P, 6 * P, NO - 1), (6 * P, V_FROM, NO - 1)):
                     piece = rt[l][:, 0:blocks, b0:b1]
                     nc.scalar.activation(out=piece, in_=piece, func=ACT.Square)
 
@@ -306,8 +306,6 @@ def tile_relationembedding_kernel(tc, sbj_vec, obj_vec, W1, b1, W2, b2, label_ve
 
             with tc.manual_schedule():
                 for i in range(-2, L + 1):
-                    if 0 <= i + 1 < L:
-                        squares_v(i + 1)
                     if i + 2 < L:
                         for c in range(3):
                             pass1(i + 2, c)
@@ -318,6 +316,7 @@ def tile_relationembedding_kernel(tc, sbj_vec, obj_vec, W1, b1, W2, b2, label_ve
                     if i - 1 >= 0:
                         drain(i - 1)
                     if 0 <= i + 1 < L:
+                        squares_v(i + 1)
                         squares_g(i + 1)
                         squares_s(i + 1)
                     if i + 2 < L:

@@ -23,7 +23,7 @@ NO = DO // P
 
 FLOPS = 2 * B * 2 * DH * DO + 2 * B * DO * DO + 4 * B * L * DO
 
-V_FROM = 856
+SQ_B = 7 * 128
 BURST_EVERY = 4
 TINY = 1e-30
 LATE = 16
@@ -224,16 +224,16 @@ def tile_relationembedding_kernel(tc, sbj_vec, obj_vec, W1, b1, W2, b2, label_ve
 
         with tc.tile_pool(name="pair", bufs=1) as pair, tc.tile_pool(name="rp", bufs=4) as rp, tc.tile_pool(
             name="gq", bufs=4
-        ) as gq, tc.psum_pool(name="pb", bufs=6) as pb:
+        ) as gq, tc.psum_pool(name="pb", bufs=8) as pb:
             tot = pair.tile([P, L, NB], F32, name="tot")
-            kp = pb.tile([P, HB], F32, name="kp", tag="kp", bufs=1)
+            stats = pair.tile([P, L, 4, 3], F32, name="stats")
             rt = {}
             gs = {}
             banks = {}
 
-            def keeper():
+            def keeper(bank):
                 nc.tensor.matmul_mx(
-                    out=kp[:],
+                    out=bank,
                     lhsT=w2codes[:, 0, 0:P].bitcast(FP8X4),
                     lhsT_scale=w2scales[:, 0, 0:P],
                     rhs=hcodes[:, 0, 0:HB].bitcast(FP8X4),
@@ -254,51 +254,62 @@ def tile_relationembedding_kernel(tc, sbj_vec, obj_vec, W1, b1, W2, b2, label_ve
                     op1=ALU.min,
                 )
 
-            def squares_v(l):
-                piece = rt[l][:, 0 : NO - 1, V_FROM:B]
-                nc.vector.tensor_tensor(out=piece, in0=piece, in1=piece, op=ALU.mult)
-
             def gate(l):
-                gs[l] = gq.tile([P, HB], F32, name="gs", tag="gs")
+                gs[l] = gq.tile([P, SQ_B], F32, name="gs", tag="gs")
                 nc.vector.memset(gs[l][:, 0:1], 0.0)
 
             def squares_g(l):
-                nc.gpsimd.tensor_tensor(out=gs[l][:], in0=rt[l][:, NO - 1, HB:B], in1=rt[l][:, NO - 1, HB:B], op=ALU.mult)
+                nc.gpsimd.tensor_tensor(out=gs[l][:], in0=rt[l][:, NO - 1, 0:SQ_B], in1=rt[l][:, NO - 1, 0:SQ_B], op=ALU.mult)
 
             def squares_s(l):
-                for b0, b1, blocks in ((0, 2 * P, NO), (2 * P, 4 * P, NO), (4 * P, 6 * P, NO - 1), (6 * P, V_FROM, NO - 1)):
-                    piece = rt[l][:, 0:blocks, b0:b1]
+                for b0 in range(0, SQ_B, 2 * P):
+                    piece = rt[l][:, 0 : NO - 1, b0 : min(b0 + 2 * P, SQ_B)]
                     nc.scalar.activation(out=piece, in_=piece, func=ACT.Square)
 
             def turn(l):
+                for q in range(4):
+                    banks[(l, q)] = pb.tile([P, 4, P], F32, name="bank", tag="bank")
                 if l % BURST_EVERY == 0:
                     for i in range(3):
-                        keeper()
-                for q in range(2):
-                    banks[(l, q)] = pb.tile([P, 4, P], F32, name="bank", tag="bank")
+                        keeper(banks[(l, 0)][:].rearrange("p k b -> p (k b)"))
                 for k in range(4):
                     for c in range(NO):
                         for q in range(2):
                             bb = 2 * k + q
-                            block = rt[l][:, c, bb * P : (bb + 1) * P]
-                            if c == NO - 1 and bb * P >= HB:
-                                block = gs[l][:, bb * P - HB : (bb + 1) * P - HB]
-                            nc.tensor.matmul(
-                                out=banks[(l, q)][:, k, :],
-                                lhsT=block,
-                                rhs=ident_f[:],
-                                is_transpose=True,
-                                start=(c == 0),
-                                stop=(c == NO - 1),
-                            )
+                            if bb == NB - 1:
+                                nc.tensor.transpose(banks[(l, 2 + c // 4)][:, c % 4, :], rt[l][:, c, bb * P : (bb + 1) * P], ident_f[:])
+                            else:
+                                block = rt[l][:, c, bb * P : (bb + 1) * P]
+                                if c == NO - 1:
+                                    block = gs[l][:, bb * P : (bb + 1) * P]
+                                nc.tensor.matmul(
+                                    out=banks[(l, q)][:, k, :],
+                                    lhsT=block,
+                                    rhs=ident_f[:],
+                                    is_transpose=True,
+                                    start=(c == 0),
+                                    stop=(c == NO - 1),
+                                )
 
             def drain(l):
-                for q in range(2):
-                    nc.vector.tensor_reduce(out=tot[:, l, q:NB:2], in_=banks[(l, q)][:], axis=AX.X, op=ALU.add)
+                nc.vector.tensor_reduce(out=tot[:, l, 0:NB:2], in_=banks[(l, 0)][:], axis=AX.X, op=ALU.add)
+                nc.vector.tensor_reduce(out=tot[:, l, 1 : NB - 1 : 2], in_=banks[(l, 1)][:, 0:3, :], axis=AX.X, op=ALU.add)
+                for j in range(2):
+                    nc.vector.bn_stats(
+                        out=stats[:, l, 2 * j : 2 * j + 2, :].rearrange("p a s -> p (a s)"),
+                        in_=banks[(l, 2 + j)][:].rearrange("p k b -> p (k b)"),
+                    )
 
             res = pair.tile([P, NB, L], F32, name="res")
+            msq = pair.tile([P, L, 4], F32, name="msq")
 
             def finish(l0, l1):
+                mean = stats[:, l0:l1, :, 1]
+                nc.vector.tensor_tensor(out=msq[:, l0:l1, :], in0=mean, in1=mean, op=ALU.mult)
+                nc.vector.scalar_tensor_tensor(
+                    out=msq[:, l0:l1, :], in0=msq[:, l0:l1, :], scalar=float(HB // 2), in1=stats[:, l0:l1, :, 2], op0=ALU.mult, op1=ALU.add
+                )
+                nc.vector.tensor_reduce(out=tot[:, l0:l1, NB - 1], in_=msq[:, l0:l1, :], axis=AX.X, op=ALU.add)
                 nc.vector.tensor_scalar_max(out=tot[:, l0:l1, :], in0=tot[:, l0:l1, :], scalar1=TINY)
                 nc.scalar.activation(out=res[:, :, l0:l1], in_=tot[:, l0:l1, :].rearrange("p l k -> p k l"), func=ACT.Sqrt)
                 nc.vector.tensor_scalar_mul(out=res[:, :, l0:l1], in0=res[:, :, l0:l1], scalar1=-1.0)
@@ -316,7 +327,6 @@ def tile_relationembedding_kernel(tc, sbj_vec, obj_vec, W1, b1, W2, b2, label_ve
                     if i - 1 >= 0:
                         drain(i - 1)
                     if 0 <= i + 1 < L:
-                        squares_v(i + 1)
                         squares_g(i + 1)
                         squares_s(i + 1)
                     if i + 2 < L:

import concourse.mybir as mybir
from concourse.masks import make_identity

F32 = mybir.dt.float32
BF16 = mybir.dt.bfloat16
U32 = mybir.dt.uint32
U8 = mybir.dt.uint8
FP8X4 = mybir.dt.float8_e4m3fn_x4
ALU = mybir.AluOpType
ACT = mybir.ActivationFunctionType
AX = mybir.AxisListType

P = 128
B, DH, DO, L = 1024, 2048, 1024, 128
PACK = 4
KPASS = P * PACK
G1 = 2 * DH // KPASS
G2 = DO // KPASS
NB = B // P
HB = 512
NH = B // HB
NO = DO // P

FLOPS = 2 * B * 2 * DH * DO + 2 * B * DO * DO + 4 * B * L * DO

SQ_B = 7 * 128
BURST_EVERY = 4
TINY = 1e-30
LATE = 16


def tile_relationembedding_kernel(tc, sbj_vec, obj_vec, W1, b1, W2, b2, label_vecs, out):
    nc = tc.nc
    with tc.tile_pool(name="keep", bufs=1) as keep:
        ident_f = keep.tile([P, P], F32, name="ident_f")
        make_identity(nc, ident_f[:])
        ident_b = keep.tile([P, P], BF16, name="ident_b")
        make_identity(nc, ident_b[:])
        one = keep.tile([P, 1], F32, name="one")
        nc.vector.memset(one[:], 1.0)
        nc.scalar.activation(out=one[:], in_=one[:], func=ACT.Sqrt)
        biasT = keep.tile([P, 16], F32, name="biasT")
        labT = keep.tile([P, NO, L], F32, name="labT")
        embT = keep.tile([P, NO, B], F32, name="embT")
        w2codes = keep.tile([P, G2, DO], U32, name="w2codes", align_bytes=64)
        w2scales = keep.tile([P, G2, DO], U8, name="w2scales", align_bytes=64)
        hcodes = keep.tile([P, G2, B], U32, name="hcodes", align_bytes=64)
        hscales = keep.tile([P, G2, B], U8, name="hscales", align_bytes=64)

        with tc.tile_pool(name="mx", bufs=1) as mx, tc.tile_pool(name="xraw", bufs=6) as xraw, tc.tile_pool(
            name="xgrp", bufs=4
        ) as xgrp, tc.tile_pool(name="wraw", bufs=4) as wraw, tc.tile_pool(name="wgrp", bufs=4) as wgrp, tc.tile_pool(
            name="hraw", bufs=2
        ) as hraw:
            xcodes = mx.tile([P, G1, B], U32, name="xcodes", align_bytes=64)
            xscales = mx.tile([P, G1, B], U8, name="xscales", align_bytes=64)
            w1codes = mx.tile([P, G1, DO], U32, name="w1codes", align_bytes=64)
            w1scales = mx.tile([P, G1, DO], U8, name="w1scales", align_bytes=64)

            lab_sb = mx.tile([P, DO], BF16, name="lab_sb")
            nc.scalar.dma_start(out=lab_sb[:], in_=label_vecs)
            bias_rows = mx.tile([P, P], BF16, name="bias_rows")
            nc.vector.memset(bias_rows[:], 0.0)
            nc.scalar.dma_start(out=bias_rows[0:8, :], in_=b1.rearrange("(r c) -> r c", c=P))
            nc.scalar.dma_start(out=bias_rows[8:16, :], in_=b2.rearrange("(r c) -> r c", c=P))

            x_order = [(s, bb) for h in range(NH) for s in range(2) for bb in range(4 * h, 4 * h + 4)]
            xr = {}
            xg = {}

            def x_load(i):
                s, bb = x_order[i]
                xr[i] = xraw.tile([P, DH], BF16, name="xr", tag="xr")
                nc.sync.dma_start(out=xr[i][:], in_=(sbj_vec, obj_vec)[s][bb * P : (bb + 1) * P, :])
                nc.vector.tensor_scalar_max(out=xr[i][:], in0=xr[i][:], scalar1=0.0)

            def x_turn(pt, i):
                words = xr[i][:].bitcast(F32)
                for j in range(2):
                    bank = pt.tile([P, 2, 2, P], F32, name="xt", tag="xt")
                    for g2 in range(2):
                        for u in range(2):
                            c0 = 256 * (2 * j + g2) + P * u
                            nc.tensor.transpose(bank[:, g2, u, :], words[:, c0 : c0 + P], ident_f[:])
                    xg[(i, j)] = xgrp.tile([P, 2, PACK * P], BF16, name="xg", tag="xg", align_bytes=64)
                    nc.scalar.copy(
                        out=xg[(i, j)][:].bitcast(F32).rearrange("p g (b u) -> p g b u", u=2),
                        in_=bank[:].rearrange("p g u b -> p g b u"),
                    )

            def x_quant(i):
                s, bb = x_order[i]
                cols = slice(bb * P, (bb + 1) * P)
                for j in range(2):
                    for g2 in range(2):
                        g = 4 * s + 2 * j + g2
                        nc.vector.quantize_mx(
                            out=xcodes[:, g, cols].bitcast(FP8X4), scales=xscales[:, g, cols], in_=xg[(i, j)][:, g2, :]
                        )

            with tc.psum_pool(name="pt", bufs=4) as pt:
                for i in range(len(x_order) + 1):
                    if i < len(x_order):
                        x_load(i)
                        x_turn(pt, i)
                    if i >= 1:
                        x_quant(i - 1)
                tb = pt.tile([P, P], BF16, name="tb", tag="xt")
                nc.tensor.transpose(tb[:], bias_rows[:], ident_b[:])
                nc.vector.tensor_copy(out=biasT[:], in_=tb[:, 0:16])
                tl = pt.tile([P, NO, L], BF16, name="tl", tag="xt")
                for c in range(NO):
                    nc.tensor.transpose(tl[:, c, :], lab_sb[:, c * P : (c + 1) * P], ident_b[:])
                nc.vector.tensor_copy(out=labT[:], in_=tl[:])

            w1_view = W1.rearrange("(g u q e) n -> g q u (e n)", u=2, q=P, e=2)
            w2_view = W2.rearrange("(g t p) n -> g p t n", t=PACK, p=P)
            wr = {}
            wg = {}

            def w_load(g):
                wr[g] = wraw.tile([P, PACK, DO], BF16, name="wr", tag="wr")
                if g < G1:
                    nc.sync.dma_start(out=wr[g][:].rearrange("p (u e) n -> p u (e n)", e=2), in_=w1_view[g])
                else:
                    nc.sync.dma_start(out=wr[g][:], in_=w2_view[g - G1])

            def regroup(raw_view, key, on_scalar):
                wg[key] = wgrp.tile([P, HB, PACK], BF16, name="wg", tag="wg", align_bytes=64)
                dst = wg[key][:].rearrange("p (c i) t -> p c t i", i=4)
                src = raw_view.rearrange("p t (c i) -> p c t i", i=4)
                if on_scalar:
                    nc.scalar.copy(out=dst, in_=src)
                else:
                    nc.vector.tensor_copy(out=dst, in_=src)

            def quantise(key, codes, scales):
                nc.vector.quantize_mx(out=codes.bitcast(FP8X4), scales=scales, in_=wg[key][:].rearrange("p n t -> p (n t)"))

            def w_regroup(g):
                for nh in range(2):
                    regroup(wr[g][:, :, nh * HB : (nh + 1) * HB], (g, nh), nh == 1)

            def w_quant(g):
                for nh in range(2):
                    cols = slice(nh * HB, (nh + 1) * HB)
                    if g < G1:
                        quantise((g, nh), w1codes[:, g, cols], w1scales[:, g, cols])
                    else:
                        quantise((g, nh), w2codes[:, g - G1, cols], w2scales[:, g - G1, cols])

            def hidden_pass(ps, h, ob, g):
                cols = slice(h * HB, (h + 1) * HB)
                nc.tensor.matmul_mx(
                    out=ps[:],
                    lhsT=w1codes[:, g, ob * P : (ob + 1) * P].bitcast(FP8X4),
                    lhsT_scale=w1scales[:, g, ob * P : (ob + 1) * P],
                    rhs=xcodes[:, g, cols].bitcast(FP8X4),
                    rhs_scale=xscales[:, g, cols],
                    start=(g == 0),
                    stop=(g == G1 - 1),
                )

            hr = {}

            def hidden_out(ps, h, ob):
                c2, t = divmod(ob, PACK)
                if t == 0:
                    hr[(h, c2)] = hraw.tile([P, PACK, HB], BF16, name="hr", tag="hr")
                nc.scalar.activation(out=hr[(h, c2)][:, t, :], in_=ps[:], func=ACT.Relu, bias=biasT[:, ob : ob + 1], scale=1.0)

            def hidden_quant(h, c2):
                cols = slice(h * HB, (h + 1) * HB)
                regroup(hr[(h, c2)][:], ("h", h, c2), False)
                quantise(("h", h, c2), hcodes[:, c2, cols], hscales[:, c2, cols])

            def embed(pm, h):
                cols = slice(h * HB, (h + 1) * HB)
                for ob in range(NO):
                    ps = pm.tile([P, HB], F32, name="mm", tag="mm")
                    for c2 in range(G2):
                        nc.tensor.matmul_mx(
                            out=ps[:],
                            lhsT=w2codes[:, c2, ob * P : (ob + 1) * P].bitcast(FP8X4),
                            lhsT_scale=w2scales[:, c2, ob * P : (ob + 1) * P],
                            rhs=hcodes[:, c2, cols].bitcast(FP8X4),
                            rhs_scale=hscales[:, c2, cols],
                            start=(c2 == 0),
                            stop=(c2 == G2 - 1),
                        )
                    nc.scalar.activation(
                        out=embT[:, ob, cols], in_=ps[:], func=ACT.Identity, bias=biasT[:, NO + ob : NO + ob + 1], scale=1.0
                    )

            with tc.psum_pool(name="pm", bufs=8) as pm:
                acc = [pm.tile([P, HB], F32, name="mm", tag="mm") for ob in range(NO)]
                for g in range(G1 + 2):
                    if g < G1:
                        w_load(g)
                        w_regroup(g)
                    if 1 <= g <= G1:
                        w_quant(g - 1)
                    if g >= 2:
                        for ob in range(NO):
                            hidden_pass(acc[ob], 0, ob, g - 2)
                for g in range(G1, G1 + G2):
                    w_load(g)
                for ob in range(NO):
                    hidden_out(acc[ob], 0, ob)
                    if ob % PACK == PACK - 1:
                        hidden_quant(0, ob // PACK)
                for g in range(G1, G1 + G2):
                    w_regroup(g)
                    w_quant(g)
                for ob in range(NO):
                    ps = pm.tile([P, HB], F32, name="mm", tag="mm")
                    for g in range(G1):
                        hidden_pass(ps, 1, ob, g)
                    hidden_out(ps, 1, ob)
                    if ob % PACK == PACK - 1:
                        hidden_quant(1, ob // PACK)
                embed(pm, 0)
                embed(pm, 1)

        with tc.tile_pool(name="pair", bufs=1) as pair, tc.tile_pool(name="rp", bufs=4) as rp, tc.tile_pool(
            name="gq", bufs=4
        ) as gq, tc.psum_pool(name="pb", bufs=8) as pb:
            tot = pair.tile([P, L, NB], F32, name="tot")
            stats = pair.tile([P, L, 4, 3], F32, name="stats")
            rt = {}
            gs = {}
            banks = {}

            def keeper(bank):
                nc.tensor.matmul_mx(
                    out=bank,
                    lhsT=w2codes[:, 0, 0:P].bitcast(FP8X4),
                    lhsT_scale=w2scales[:, 0, 0:P],
                    rhs=hcodes[:, 0, 0:HB].bitcast(FP8X4),
                    rhs_scale=hscales[:, 0, 0:HB],
                    start=True,
                    stop=True,
                )

            def pass1(l, c):
                if c == 0:
                    rt[l] = rp.tile([P, NO, B], F32, name="r", tag="r")
                nc.vector.tensor_scalar(
                    out=rt[l][:, c, :],
                    in0=embT[:, c, :],
                    scalar1=labT[:, c, l : l + 1],
                    scalar2=0.0,
                    op0=ALU.subtract,
                    op1=ALU.min,
                )

            def gate(l):
                gs[l] = gq.tile([P, SQ_B], F32, name="gs", tag="gs")
                nc.vector.memset(gs[l][:, 0:1], 0.0)

            def squares_g(l):
                nc.gpsimd.tensor_tensor(out=gs[l][:], in0=rt[l][:, NO - 1, 0:SQ_B], in1=rt[l][:, NO - 1, 0:SQ_B], op=ALU.mult)

            def squares_s(l):
                for b0 in range(0, SQ_B, 2 * P):
                    piece = rt[l][:, 0 : NO - 1, b0 : min(b0 + 2 * P, SQ_B)]
                    nc.scalar.activation(out=piece, in_=piece, func=ACT.Square)

            def turn(l):
                for q in range(4):
                    banks[(l, q)] = pb.tile([P, 4, P], F32, name="bank", tag="bank")
                if l % BURST_EVERY == 0:
                    for i in range(3):
                        keeper(banks[(l, 0)][:].rearrange("p k b -> p (k b)"))
                for k in range(4):
                    for c in range(NO):
                        for q in range(2):
                            bb = 2 * k + q
                            if bb == NB - 1:
                                nc.tensor.transpose(banks[(l, 2 + c // 4)][:, c % 4, :], rt[l][:, c, bb * P : (bb + 1) * P], ident_f[:])
                            else:
                                block = rt[l][:, c, bb * P : (bb + 1) * P]
                                if c == NO - 1:
                                    block = gs[l][:, bb * P : (bb + 1) * P]
                                nc.tensor.matmul(
                                    out=banks[(l, q)][:, k, :],
                                    lhsT=block,
                                    rhs=ident_f[:],
                                    is_transpose=True,
                                    start=(c == 0),
                                    stop=(c == NO - 1),
                                )

            def drain(l):
                nc.vector.tensor_reduce(out=tot[:, l, 0:NB:2], in_=banks[(l, 0)][:], axis=AX.X, op=ALU.add)
                nc.vector.tensor_reduce(out=tot[:, l, 1 : NB - 1 : 2], in_=banks[(l, 1)][:, 0:3, :], axis=AX.X, op=ALU.add)
                for j in range(2):
                    nc.vector.bn_stats(
                        out=stats[:, l, 2 * j : 2 * j + 2, :].rearrange("p a s -> p (a s)"),
                        in_=banks[(l, 2 + j)][:].rearrange("p k b -> p (k b)"),
                    )

            res = pair.tile([P, NB, L], F32, name="res")
            msq = pair.tile([P, L, 4], F32, name="msq")

            def finish(l0, l1):
                mean = stats[:, l0:l1, :, 1]
                nc.vector.tensor_tensor(out=msq[:, l0:l1, :], in0=mean, in1=mean, op=ALU.mult)
                nc.vector.scalar_tensor_tensor(
                    out=msq[:, l0:l1, :], in0=msq[:, l0:l1, :], scalar=float(HB // 2), in1=stats[:, l0:l1, :, 2], op0=ALU.mult, op1=ALU.add
                )
                nc.vector.tensor_reduce(out=tot[:, l0:l1, NB - 1], in_=msq[:, l0:l1, :], axis=AX.X, op=ALU.add)
                nc.vector.tensor_scalar_max(out=tot[:, l0:l1, :], in0=tot[:, l0:l1, :], scalar1=TINY)
                nc.scalar.activation(out=res[:, :, l0:l1], in_=tot[:, l0:l1, :].rearrange("p l k -> p k l"), func=ACT.Sqrt)
                nc.vector.tensor_scalar_mul(out=res[:, :, l0:l1], in0=res[:, :, l0:l1], scalar1=-1.0)
                nc.sync.dma_start(out=out.rearrange("(k p) l -> p k l", p=P)[:, :, l0:l1], in_=res[:, :, l0:l1])

            with tc.manual_schedule():
                for i in range(-2, L + 1):
                    if i + 2 < L:
                        for c in range(3):
                            pass1(i + 2, c)
                    if 0 <= i + 1 < L:
                        gate(i + 1)
                    if i + 2 < L:
                        pass1(i + 2, 3)
                    if i - 1 >= 0:
                        drain(i - 1)
                    if 0 <= i + 1 < L:
                        squares_g(i + 1)
                        squares_s(i + 1)
                    if i + 2 < L:
                        for c in range(4, NO):
                            pass1(i + 2, c)
                    if 0 <= i + 1 < L:
                        turn(i + 1)
                    if i == L - 2:
                        finish(0, L - LATE)

            finish(L - LATE, L)
